import numpy as np
import ml_dtypes


def mxq(x, axis, fmt="e4m3"):
    dtype, down = {"e4m3": (ml_dtypes.float8_e4m3fn, 7), "e5m2": (ml_dtypes.float8_e5m2, 14)}[fmt]
    v = np.moveaxis(np.asarray(x, np.float32).astype(ml_dtypes.bfloat16).astype(np.float64), axis, -1)
    blocks = v.reshape(v.shape[:-1] + (-1, 32))
    amax = np.abs(blocks).max(-1, keepdims=True)
    byte = np.maximum(np.where(amax > 0, np.frexp(amax)[1] - 1 + 127, 0) - down, 1)
    scale = np.exp2(byte - 127.0)
    codes = (blocks / scale).astype(np.float32).astype(dtype).astype(np.float64)
    return np.moveaxis((codes * scale).reshape(v.shape), -1, axis)


WIDE = False


def mx_kscale(k):
    if not WIDE:
        return np.ones(k)
    levels = np.array([10, -10, 5, -5, 0])
    a = np.random.permutation(np.resize(levels, k // 512 * 4)).reshape(k // 512, 4)
    idx = np.arange(k)
    return np.exp2(a[idx // 512, idx % 128 // 32])


BF16 = ml_dtypes.bfloat16


def bf(x):
    return np.asarray(x, np.float32).astype(BF16)


def f64(x):
    return np.asarray(x).astype(np.float64)


B, L, D, E, W1, C, F_LEN = 8, 1024, 511, 512, 8, 128, 4
SR = 0.55
WS = 0.7
KEEP = 0.75


def setup_inputs():
    s = mx_kscale(E)
    st = np.random.standard_normal((B, L, E)) * SR
    st[..., 0] = 1.0
    return {"state": bf(st * s),
            "Wg": bf(np.random.standard_normal((C, W1, E)) * WS / np.sqrt(E) / s),
            "Mg": bf(np.random.random((C, W1, E)) < KEEP),
            "bg": bf(1.0 + 0.1 * np.random.standard_normal((C, W1)))}


def reference(state, Wg, Mg, bg):
    wm = f64(Wg) * f64(Mg)
    sq = mxq(f64(state).reshape(B * L, E), 1, "e4m3")
    wq = mxq(wm.reshape(C * W1, E), 1, "e4m3")
    h = (sq @ wq.T).reshape(B, L, C, W1) + f64(bg)
    return np.prod(h, axis=-1)

@@ -1,0 +1,221 @@
+from contextlib import ExitStack
+
+import concourse.mybir as mybir
+from concourse.masks import make_identity
+
+FP8X4 = mybir.dt.float8_e4m3fn_x4
+BF16 = mybir.dt.bfloat16
+F32 = mybir.dt.float32
+U32 = mybir.dt.uint32
+U8 = mybir.dt.uint8
+ADD = mybir.AluOpType.add
+MULT = mybir.AluOpType.mult
+IDENTITY = mybir.ActivationFunctionType.Identity
+
+P = 128
+E = 512
+WORDS = E // 2
+TOKENS = 8 * 1024
+FORMS = 8
+CHAINS = 3
+ROUND = 512
+ROUNDS = TOKENS // ROUND
+ROUND_BLOCKS = ROUND // P
+PAIR = 2
+AHEAD = 3
+EARLY_ROUNDS = AHEAD - 1
+BEHIND = 2
+PARTIALS = 9
+
+FLOPS = 2 * TOKENS * P * FORMS * E
+
+
+def tile_ac_filter_prenorm_net_nd_pa_t_kernel(tc, state, Wg, Mg, bg, out):
+    nc = tc.nc
+
+    state_rounds = state.flatten_outer_dims().rearrange("(r p a) e -> r p (a e)", p=P, a=ROUND_BLOCKS)
+    out_rounds = out.flatten_outer_dims().rearrange("(r p a) c -> r p (a c)", p=P, a=ROUND_BLOCKS)
+    wg_rows = Wg.rearrange("c j e -> c (j e)")
+    mg_rows = Mg.rearrange("c j e -> c (j e)")
+
+    with ExitStack() as ctx:
+        keep = ctx.enter_context(tc.tile_pool(name="keep", bufs=1))
+        stage = ctx.enter_context(tc.tile_pool(name="stage", bufs=2))
+        psum = ctx.enter_context(tc.psum_pool(name="psum", bufs=1))
+        ctx.enter_context(tc.manual_schedule())
+
+        bg_sb = keep.tile([P, FORMS], BF16)
+        nc.scalar.dma_start(out=bg_sb[:], in_=bg)
+        state_sb = []
+        wg_sb = []
+        mg_sb = []
+
+        def load_state(r):
+            state_round = keep.tile([P, ROUND_BLOCKS * E], BF16, name="state_%d" % r)
+            nc.sync.dma_start(out=state_round[:], in_=state_rounds[r])
+            state_sb.append(state_round)
+
+        load_state(0)
+        for pair in range(FORMS // PAIR):
+            cols = slice(pair * PAIR * E, (pair + 1) * PAIR * E)
+            wg_pair = keep.tile([P, PAIR * E], BF16, name="wg_%d" % pair)
+            mg_pair = keep.tile([P, PAIR * E], BF16, name="mg_%d" % pair)
+            nc.sync.dma_start(out=wg_pair[:], in_=wg_rows[:, cols])
+            nc.sync.dma_start(out=mg_pair[:], in_=mg_rows[:, cols])
+            wg_sb.append(wg_pair)
+            mg_sb.append(mg_pair)
+        for r in range(1, ROUNDS):
+            load_state(r)
+
+        identity = keep.tile([P, P], F32)
+        make_identity(nc, identity[:])
+        bias = keep.tile([P, FORMS], F32)
+        nc.scalar.activation(out=bias[:], in_=bg_sb[:], func=IDENTITY)
+
+        def transpose_pair(words):
+            flipped = psum.tile([P, 2, PAIR * P], F32, tag="flipped", bufs=2)
+            for b in range(PAIR):
+                for u in range(2):
+                    nc.tensor.transpose(
+                        flipped[:, u, b * P : (b + 1) * P],
+                        words[:, b * WORDS + u * P : b * WORDS + (u + 1) * P],
+                        identity[:],
+                    )
+            return flipped
+
+        def regroup_pair(flipped, grouped):
+            nc.scalar.copy(
+                out=grouped.bitcast(F32).rearrange("p (n u) -> p n u", u=2),
+                in_=flipped[:].rearrange("p u n -> p n u"),
+            )
+
+        flipped_state = {}
+        grouped_state = {}
+        quantised = {}
+        chains = {}
+        results = {}
+
+        def is_round(r):
+            return 0 <= r < ROUNDS
+
+        def transpose_state(r):
+            words = state_sb[r][:].bitcast(F32)
+            half_words = PAIR * WORDS
+            flipped_state[r] = [transpose_pair(words[:, h * half_words : (h + 1) * half_words]) for h in range(2)]
+            grouped_state[r] = stage.tile([P, ROUND * 4], BF16, align_bytes=64, tag="grouped", name="grouped")
+
+        def regroup_state(r, h):
+            half_cols = ROUND * 4 // 2
+            regroup_pair(flipped_state[r][h], grouped_state[r][:, h * half_cols : (h + 1) * half_cols])
+
+        def quantise_state(r):
+            codes = stage.tile([P, ROUND], U32, align_bytes=64, tag="x_codes", bufs=3)
+            scales = stage.tile([P, ROUND], U8, align_bytes=64, tag="x_scales", bufs=3)
+            nc.vector.quantize_mx(out=codes[:].bitcast(FP8X4), scales=scales[:], in_=grouped_state[r][:])
+            quantised[r] = (codes, scales)
+
+        def form(r, j, tag, bufs):
+            bank = psum.tile([P, ROUND], F32, tag=tag, bufs=bufs)
+            codes, scales = quantised[r]
+            cols = slice(j * P, (j + 1) * P)
+            nc.tensor.matmul_mx(
+                out=bank[:],
+                lhsT=w_codes[:, cols].bitcast(FP8X4),
+                lhsT_scale=w_scales[:, cols],
+                rhs=codes[:].bitcast(FP8X4),
+                rhs_scale=scales[:],
+                start=True,
+                stop=True,
+            )
+            return bank
+
+        def partial():
+            return stage.tile([P, ROUND], F32, tag="partial", bufs=3 * PARTIALS, name="partial")
+
+        def begin(r, k, j):
+            if is_round(r):
+                bank = form(r, j, "scalar_form", 2)
+                chains[(r, k)] = partial()
+                nc.scalar.activation(
+                    out=chains[(r, k)][:], in_=bank[:], func=IDENTITY, bias=bias[:, j : j + 1], scale=1.0
+                )
+
+        def extend(r, k, j):
+            if is_round(r):
+                bank = form(r, j, "vector_form", 3)
+                longer = partial()
+                nc.vector.scalar_tensor_tensor(
+                    out=longer[:], in0=bank[:], scalar=bias[:, j : j + 1], in1=chains[(r, k)][:], op0=ADD, op1=MULT
+                )
+                chains[(r, k)] = longer
+
+        def join(r):
+            if is_round(r):
+                two = partial()
+                nc.gpsimd.tensor_tensor(out=two[:], in0=chains[(r, 2)][:], in1=chains[(r, 0)][:], op=MULT)
+                results[r] = stage.tile([P, ROUND], F32, tag="result", bufs=BEHIND + 1, name="result")
+                nc.gpsimd.tensor_tensor(out=results[r][:], in0=two[:], in1=chains[(r, 1)][:], op=MULT)
+
+        def store(r):
+            if is_round(r):
+                back = psum.tile([P, ROUND], F32, tag="back", bufs=1)
+                for a in range(ROUND_BLOCKS):
+                    cols = slice(a * P, (a + 1) * P)
+                    nc.tensor.transpose(back[:, cols], results[r][:, cols], identity[:])
+                out_sb = stage.tile([P, ROUND], F32)
+                nc.scalar.copy(out=out_sb[:], in_=back[:])
+                nc.sync.dma_start(out=out_rounds[r], in_=out_sb[:])
+
+        def tick(t):
+            fresh = t + AHEAD
+            begin(t + 1, 0, 0)
+            if EARLY_ROUNDS <= fresh - 1 < ROUNDS:
+                regroup_state(fresh - 1, 1)
+            extend(t, 0, 1)
+            begin(t + 1, 1, 2)
+            extend(t, 1, 3)
+            begin(t + 1, 2, 4)
+            extend(t, 2, 5)
+            if EARLY_ROUNDS <= fresh - 1 < ROUNDS:
+                quantise_state(fresh - 1)
+            extend(t, 0, 6)
+            extend(t, 1, 7)
+            join(t)
+            store(t - BEHIND)
+            if fresh < ROUNDS:
+                transpose_state(fresh)
+                regroup_state(fresh, 0)
+
+        def prepare_state(r):
+            transpose_state(r)
+            regroup_state(r, 0)
+            regroup_state(r, 1)
+            quantise_state(r)
+
+        prepare_state(0)
+
+        w_codes = keep.tile([P, FORMS * P], U32, align_bytes=64)
+        w_scales = keep.tile([P, FORMS * P], U8, align_bytes=64)
+        w_grouped = []
+
+        def quantise_weights(pair):
+            cols = slice(pair * PAIR * P, (pair + 1) * PAIR * P)
+            nc.vector.quantize_mx(
+                out=w_codes[:, cols].bitcast(FP8X4), scales=w_scales[:, cols], in_=w_grouped[pair][:]
+            )
+
+        for pair in range(FORMS // PAIR):
+            masked = keep.tile([P, PAIR * E], BF16, name="masked_%d" % pair)
+            nc.vector.tensor_tensor(out=masked[:], in0=wg_sb[pair][:], in1=mg_sb[pair][:], op=MULT)
+            grouped = keep.tile([P, PAIR * P * 4], BF16, align_bytes=64, name="w_grouped_%d" % pair)
+            regroup_pair(transpose_pair(masked[:].bitcast(F32)), grouped[:])
+            w_grouped.append(grouped)
+            if pair > 0:
+                quantise_weights(pair - 1)
+        quantise_weights(FORMS // PAIR - 1)
+
+        for r in range(1, EARLY_ROUNDS):
+            prepare_state(r)
+
+        for t in range(-1, ROUNDS + BEHIND):
+            tick(t)

@@ -17,15 +17,20 @@ E = 512
 WORDS = E // 2
 TOKENS = 8 * 1024
 FORMS = 8
-CHAINS = 3
 ROUND = 512
 ROUNDS = TOKENS // ROUND
 ROUND_BLOCKS = ROUND // P
 PAIR = 2
+PAIR_ROWS = PAIR * P
+WEIGHT_PAIRS = FORMS // PAIR
+BANKS = 8
 AHEAD = 3
-EARLY_ROUNDS = AHEAD - 1
 BEHIND = 2
 PARTIALS = 9
+
+CHAIN_A = (0, 1, 2, 3)
+CHAIN_B = (4, 5)
+CHAIN_C = (6, 7)
 
 FLOPS = 2 * TOKENS * P * FORMS * E
 
@@ -41,7 +46,7 @@ def tile_ac_filter_prenorm_net_nd_pa_t_kernel(tc, state, Wg, Mg, bg, out):
     with ExitStack() as ctx:
         keep = ctx.enter_context(tc.tile_pool(name="keep", bufs=1))
         stage = ctx.enter_context(tc.tile_pool(name="stage", bufs=2))
-        psum = ctx.enter_context(tc.psum_pool(name="psum", bufs=1))
+        psum = ctx.enter_context(tc.psum_pool(name="psum", bufs=BANKS))
         ctx.enter_context(tc.manual_schedule())
 
         bg_sb = keep.tile([P, FORMS], BF16)
@@ -56,7 +61,7 @@ def tile_ac_filter_prenorm_net_nd_pa_t_kernel(tc, state, Wg, Mg, bg, out):
             state_sb.append(state_round)
 
         load_state(0)
-        for pair in range(FORMS // PAIR):
+        for pair in range(WEIGHT_PAIRS):
             cols = slice(pair * PAIR * E, (pair + 1) * PAIR * E)
             wg_pair = keep.tile([P, PAIR * E], BF16, name="wg_%d" % pair)
             mg_pair = keep.tile([P, PAIR * E], BF16, name="mg_%d" % pair)
@@ -72,12 +77,16 @@ def tile_ac_filter_prenorm_net_nd_pa_t_kernel(tc, state, Wg, Mg, bg, out):
         bias = keep.tile([P, FORMS], F32)
         nc.scalar.activation(out=bias[:], in_=bg_sb[:], func=IDENTITY)
 
+        def next_bank():
+            bank = psum.tile([P, ROUND], F32, tag="bank")
+            return bank
+
         def transpose_pair(words):
-            flipped = psum.tile([P, 2, PAIR * P], F32, tag="flipped", bufs=2)
+            flipped = next_bank()
             for b in range(PAIR):
                 for u in range(2):
                     nc.tensor.transpose(
-                        flipped[:, u, b * P : (b + 1) * P],
+                        flipped[:, u * PAIR_ROWS + b * P : u * PAIR_ROWS + (b + 1) * P],
                         words[:, b * WORDS + u * P : b * WORDS + (u + 1) * P],
                         identity[:],
                     )
@@ -86,7 +95,7 @@ def tile_ac_filter_prenorm_net_nd_pa_t_kernel(tc, state, Wg, Mg, bg, out):
         def regroup_pair(flipped, grouped):
             nc.scalar.copy(
                 out=grouped.bitcast(F32).rearrange("p (n u) -> p n u", u=2),
-                in_=flipped[:].rearrange("p u n -> p n u"),
+                in_=flipped[:].rearrange("p (u n) -> p n u", u=2),
             )
 
         flipped_state = {}
@@ -94,28 +103,34 @@ def tile_ac_filter_prenorm_net_nd_pa_t_kernel(tc, state, Wg, Mg, bg, out):
         quantised = {}
         chains = {}
         results = {}
+        backs = {}
 
         def is_round(r):
             return 0 <= r < ROUNDS
 
         def transpose_state(r):
-            words = state_sb[r][:].bitcast(F32)
-            half_words = PAIR * WORDS
-            flipped_state[r] = [transpose_pair(words[:, h * half_words : (h + 1) * half_words]) for h in range(2)]
-            grouped_state[r] = stage.tile([P, ROUND * 4], BF16, align_bytes=64, tag="grouped", name="grouped")
+            if is_round(r):
+                words = state_sb[r][:].bitcast(F32)
+                half_words = PAIR * WORDS
+                flipped_state[r] = [transpose_pair(words[:, h * half_words : (h + 1) * half_words]) for h in range(2)]
 
-        def regroup_state(r, h):
-            half_cols = ROUND * 4 // 2
-            regroup_pair(flipped_state[r][h], grouped_state[r][:, h * half_cols : (h + 1) * half_cols])
+        def regroup_state(r):
+            if is_round(r):
+                grouped = stage.tile([P, ROUND * 4], BF16, align_bytes=64)
+                half_cols = PAIR_ROWS * 4
+                for h in range(2):
+                    regroup_pair(flipped_state[r][h], grouped[:, h * half_cols : (h + 1) * half_cols])
+                grouped_state[r] = grouped
 
         def quantise_state(r):
-            codes = stage.tile([P, ROUND], U32, align_bytes=64, tag="x_codes", bufs=3)
-            scales = stage.tile([P, ROUND], U8, align_bytes=64, tag="x_scales", bufs=3)
-            nc.vector.quantize_mx(out=codes[:].bitcast(FP8X4), scales=scales[:], in_=grouped_state[r][:])
-            quantised[r] = (codes, scales)
+            if is_round(r):
+                codes = stage.tile([P, ROUND], U32, align_bytes=64, tag="x_codes", bufs=AHEAD + 1)
+                scales = stage.tile([P, ROUND], U8, align_bytes=64, tag="x_scales", bufs=AHEAD + 1)
+                nc.vector.quantize_mx(out=codes[:].bitcast(FP8X4), scales=scales[:], in_=grouped_state[r][:])
+                quantised[r] = (codes, scales)
 
-        def form(r, j, tag, bufs):
-            bank = psum.tile([P, ROUND], F32, tag=tag, bufs=bufs)
+        def form(r, j):
+            bank = next_bank()
             codes, scales = quantised[r]
             cols = slice(j * P, (j + 1) * P)
             nc.tensor.matmul_mx(
@@ -130,92 +145,101 @@ def tile_ac_filter_prenorm_net_nd_pa_t_kernel(tc, state, Wg, Mg, bg, out):
             return bank
 
         def partial():
-            return stage.tile([P, ROUND], F32, tag="partial", bufs=3 * PARTIALS, name="partial")
+            product = stage.tile([P, ROUND], F32, tag="partial", bufs=3 * PARTIALS)
+            return product
 
-        def begin(r, k, j):
+        def begin(r, chain):
             if is_round(r):
-                bank = form(r, j, "scalar_form", 2)
-                chains[(r, k)] = partial()
+                j = chain[0]
+                bank = form(r, j)
+                chains[(r, chain)] = partial()
                 nc.scalar.activation(
-                    out=chains[(r, k)][:], in_=bank[:], func=IDENTITY, bias=bias[:, j : j + 1], scale=1.0
+                    out=chains[(r, chain)][:], in_=bank[:], func=IDENTITY, bias=bias[:, j : j + 1], scale=1.0
                 )
 
-        def extend(r, k, j):
+        def extend(r, chain, i):
             if is_round(r):
-                bank = form(r, j, "vector_form", 3)
+                j = chain[i]
+                bank = form(r, j)
                 longer = partial()
                 nc.vector.scalar_tensor_tensor(
-                    out=longer[:], in0=bank[:], scalar=bias[:, j : j + 1], in1=chains[(r, k)][:], op0=ADD, op1=MULT
+                    out=longer[:], in0=bank[:], scalar=bias[:, j : j + 1], in1=chains[(r, chain)][:], op0=ADD, op1=MULT
                 )
-                chains[(r, k)] = longer
+                chains[(r, chain)] = longer
 
-        def join(r):
+        def join_short_chains(r):
             if is_round(r):
-                two = partial()
-                nc.gpsimd.tensor_tensor(out=two[:], in0=chains[(r, 2)][:], in1=chains[(r, 0)][:], op=MULT)
-                results[r] = stage.tile([P, ROUND], F32, tag="result", bufs=BEHIND + 1, name="result")
-                nc.gpsimd.tensor_tensor(out=results[r][:], in0=two[:], in1=chains[(r, 1)][:], op=MULT)
+                joined = partial()
+                nc.gpsimd.tensor_tensor(
+                    out=joined[:], in0=chains[(r, CHAIN_B)][:], in1=chains[(r, CHAIN_C)][:], op=MULT
+                )
+                chains[(r, CHAIN_B)] = joined
 
-        def store(r):
+        def join_all(r):
             if is_round(r):
-                back = psum.tile([P, ROUND], F32, tag="back", bufs=1)
+                result = stage.tile([P, ROUND], F32, bufs=BEHIND + 2)
+                nc.gpsimd.tensor_tensor(
+                    out=result[:], in0=chains[(r, CHAIN_B)][:], in1=chains[(r, CHAIN_A)][:], op=MULT
+                )
+                results[r] = result
+
+        def transpose_result(r):
+            if is_round(r):
+                backs[r] = next_bank()
                 for a in range(ROUND_BLOCKS):
                     cols = slice(a * P, (a + 1) * P)
-                    nc.tensor.transpose(back[:, cols], results[r][:, cols], identity[:])
-                out_sb = stage.tile([P, ROUND], F32)
-                nc.scalar.copy(out=out_sb[:], in_=back[:])
+                    nc.tensor.transpose(backs[r][:, cols], results[r][:, cols], identity[:])
+
+        def store_result(r):
+            if is_round(r):
+                out_sb = stage.tile([P, ROUND], F32, bufs=3)
+                nc.scalar.copy(out=out_sb[:], in_=backs[r][:])
                 nc.sync.dma_start(out=out_rounds[r], in_=out_sb[:])
-
-        def tick(t):
-            fresh = t + AHEAD
-            begin(t + 1, 0, 0)
-            if EARLY_ROUNDS <= fresh - 1 < ROUNDS:
-                regroup_state(fresh - 1, 1)
-            extend(t, 0, 1)
-            begin(t + 1, 1, 2)
-            extend(t, 1, 3)
-            begin(t + 1, 2, 4)
-            extend(t, 2, 5)
-            if EARLY_ROUNDS <= fresh - 1 < ROUNDS:
-                quantise_state(fresh - 1)
-            extend(t, 0, 6)
-            extend(t, 1, 7)
-            join(t)
-            store(t - BEHIND)
-            if fresh < ROUNDS:
-                transpose_state(fresh)
-                regroup_state(fresh, 0)
-
-        def prepare_state(r):
-            transpose_state(r)
-            regroup_state(r, 0)
-            regroup_state(r, 1)
-            quantise_state(r)
-
-        prepare_state(0)
 
         w_codes = keep.tile([P, FORMS * P], U32, align_bytes=64)
         w_scales = keep.tile([P, FORMS * P], U8, align_bytes=64)
         w_grouped = []
+        quantise_lag = 2
 
         def quantise_weights(pair):
-            cols = slice(pair * PAIR * P, (pair + 1) * PAIR * P)
+            cols = slice(pair * PAIR_ROWS, (pair + 1) * PAIR_ROWS)
             nc.vector.quantize_mx(
                 out=w_codes[:, cols].bitcast(FP8X4), scales=w_scales[:, cols], in_=w_grouped[pair][:]
             )
 
-        for pair in range(FORMS // PAIR):
+        transpose_state(0)
+        regroup_state(0)
+        for pair in range(WEIGHT_PAIRS):
             masked = keep.tile([P, PAIR * E], BF16, name="masked_%d" % pair)
             nc.vector.tensor_tensor(out=masked[:], in0=wg_sb[pair][:], in1=mg_sb[pair][:], op=MULT)
-            grouped = keep.tile([P, PAIR * P * 4], BF16, align_bytes=64, name="w_grouped_%d" % pair)
+            if pair == 0:
+                quantise_state(0)
+            grouped = keep.tile([P, PAIR_ROWS * 4], BF16, align_bytes=64, name="w_grouped_%d" % pair)
             regroup_pair(transpose_pair(masked[:].bitcast(F32)), grouped[:])
             w_grouped.append(grouped)
-            if pair > 0:
-                quantise_weights(pair - 1)
-        quantise_weights(FORMS // PAIR - 1)
-
-        for r in range(1, EARLY_ROUNDS):
-            prepare_state(r)
+            if pair >= quantise_lag:
+                quantise_weights(pair - quantise_lag)
+        for pair in range(WEIGHT_PAIRS - quantise_lag, WEIGHT_PAIRS):
+            quantise_weights(pair)
+        for r in range(1, AHEAD - 1):
+            transpose_state(r)
+            regroup_state(r)
+            quantise_state(r)
 
         for t in range(-1, ROUNDS + BEHIND):
-            tick(t)
+            extend(t, CHAIN_C, 1)
+            if t >= 0:
+                quantise_state(t + AHEAD - 1)
+            join_short_chains(t)
+            begin(t + 1, CHAIN_A)
+            extend(t, CHAIN_A, 3)
+            join_all(t)
+            begin(t + 1, CHAIN_B)
+            extend(t + 1, CHAIN_A, 1)
+            begin(t + 1, CHAIN_C)
+            extend(t + 1, CHAIN_B, 1)
+            transpose_result(t - BEHIND)
+            transpose_state(t + AHEAD)
+            store_result(t - BEHIND)
+            regroup_state(t + AHEAD)
+            extend(t + 1, CHAIN_A, 2)

@@ -193,7 +193,10 @@ def tile_ac_filter_prenorm_net_nd_pa_t_kernel(tc, state, Wg, Mg, bg, out):
         def store_result(r):
             if is_round(r):
                 out_sb = stage.tile([P, ROUND], F32, bufs=3)
-                nc.scalar.copy(out=out_sb[:], in_=backs[r][:])
+                if r % 2 == 0:
+                    nc.scalar.copy(out=out_sb[:], in_=backs[r][:])
+                else:
+                    nc.vector.tensor_copy(out=out_sb[:], in_=backs[r][:])
                 nc.sync.dma_start(out=out_rounds[r], in_=out_sb[:])
 
         w_codes = keep.tile([P, FORMS * P], U32, align_bytes=64)

from contextlib import ExitStack

import concourse.mybir as mybir
from concourse.masks import make_identity

FP8X4 = mybir.dt.float8_e4m3fn_x4
BF16 = mybir.dt.bfloat16
F32 = mybir.dt.float32
U32 = mybir.dt.uint32
U8 = mybir.dt.uint8
ADD = mybir.AluOpType.add
MULT = mybir.AluOpType.mult
IDENTITY = mybir.ActivationFunctionType.Identity

P = 128
E = 512
WORDS = E // 2
TOKENS = 8 * 1024
FORMS = 8
ROUND = 512
ROUNDS = TOKENS // ROUND
ROUND_BLOCKS = ROUND // P
PAIR = 2
PAIR_ROWS = PAIR * P
WEIGHT_PAIRS = FORMS // PAIR
BANKS = 8
AHEAD = 3
BEHIND = 2
PARTIALS = 9

CHAIN_A = (0, 1, 2, 3)
CHAIN_B = (4, 5)
CHAIN_C = (6, 7)

FLOPS = 2 * TOKENS * P * FORMS * E


def tile_ac_filter_prenorm_net_nd_pa_t_kernel(tc, state, Wg, Mg, bg, out):
    nc = tc.nc

    state_rounds = state.flatten_outer_dims().rearrange("(r p a) e -> r p (a e)", p=P, a=ROUND_BLOCKS)
    out_rounds = out.flatten_outer_dims().rearrange("(r p a) c -> r p (a c)", p=P, a=ROUND_BLOCKS)
    wg_rows = Wg.rearrange("c j e -> c (j e)")
    mg_rows = Mg.rearrange("c j e -> c (j e)")

    with ExitStack() as ctx:
        keep = ctx.enter_context(tc.tile_pool(name="keep", bufs=1))
        stage = ctx.enter_context(tc.tile_pool(name="stage", bufs=2))
        psum = ctx.enter_context(tc.psum_pool(name="psum", bufs=BANKS))
        ctx.enter_context(tc.manual_schedule())

        bg_sb = keep.tile([P, FORMS], BF16)
        nc.scalar.dma_start(out=bg_sb[:], in_=bg)
        state_sb = []
        wg_sb = []
        mg_sb = []

        def load_state(r):
            state_round = keep.tile([P, ROUND_BLOCKS * E], BF16, name="state_%d" % r)
            nc.sync.dma_start(out=state_round[:], in_=state_rounds[r])
            state_sb.append(state_round)

        load_state(0)
        for pair in range(WEIGHT_PAIRS):
            cols = slice(pair * PAIR * E, (pair + 1) * PAIR * E)
            wg_pair = keep.tile([P, PAIR * E], BF16, name="wg_%d" % pair)
            mg_pair = keep.tile([P, PAIR * E], BF16, name="mg_%d" % pair)
            nc.sync.dma_start(out=wg_pair[:], in_=wg_rows[:, cols])
            nc.sync.dma_start(out=mg_pair[:], in_=mg_rows[:, cols])
            wg_sb.append(wg_pair)
            mg_sb.append(mg_pair)
        for r in range(1, ROUNDS):
            load_state(r)

        identity = keep.tile([P, P], F32)
        make_identity(nc, identity[:])
        bias = keep.tile([P, FORMS], F32)
        nc.scalar.activation(out=bias[:], in_=bg_sb[:], func=IDENTITY)

        def next_bank():
            bank = psum.tile([P, ROUND], F32, tag="bank")
            return bank

        def transpose_pair(words):
            flipped = next_bank()
            for b in range(PAIR):
                for u in range(2):
                    nc.tensor.transpose(
                        flipped[:, u * PAIR_ROWS + b * P : u * PAIR_ROWS + (b + 1) * P],
                        words[:, b * WORDS + u * P : b * WORDS + (u + 1) * P],
                        identity[:],
                    )
            return flipped

        def regroup_pair(flipped, grouped):
            nc.scalar.copy(
                out=grouped.bitcast(F32).rearrange("p (n u) -> p n u", u=2),
                in_=flipped[:].rearrange("p (u n) -> p n u", u=2),
            )

        flipped_state = {}
        grouped_state = {}
        quantised = {}
        chains = {}
        results = {}
        backs = {}

        def is_round(r):
            return 0 <= r < ROUNDS

        def transpose_state(r):
            if is_round(r):
                words = state_sb[r][:].bitcast(F32)
                half_words = PAIR * WORDS
                flipped_state[r] = [transpose_pair(words[:, h * half_words : (h + 1) * half_words]) for h in range(2)]

        def regroup_state(r):
            if is_round(r):
                grouped = stage.tile([P, ROUND * 4], BF16, align_bytes=64)
                half_cols = PAIR_ROWS * 4
                for h in range(2):
                    regroup_pair(flipped_state[r][h], grouped[:, h * half_cols : (h + 1) * half_cols])
                grouped_state[r] = grouped

        def quantise_state(r):
            if is_round(r):
                codes = stage.tile([P, ROUND], U32, align_bytes=64, tag="x_codes", bufs=AHEAD + 1)
                scales = stage.tile([P, ROUND], U8, align_bytes=64, tag="x_scales", bufs=AHEAD + 1)
                nc.vector.quantize_mx(out=codes[:].bitcast(FP8X4), scales=scales[:], in_=grouped_state[r][:])
                quantised[r] = (codes, scales)

        def form(r, j):
            bank = next_bank()
            codes, scales = quantised[r]
            cols = slice(j * P, (j + 1) * P)
            nc.tensor.matmul_mx(
                out=bank[:],
                lhsT=w_codes[:, cols].bitcast(FP8X4),
                lhsT_scale=w_scales[:, cols],
                rhs=codes[:].bitcast(FP8X4),
                rhs_scale=scales[:],
                start=True,
                stop=True,
            )
            return bank

        def partial():
            product = stage.tile([P, ROUND], F32, tag="partial", bufs=3 * PARTIALS)
            return product

        def begin(r, chain):
            if is_round(r):
                j = chain[0]
                bank = form(r, j)
                chains[(r, chain)] = partial()
                nc.scalar.activation(
                    out=chains[(r, chain)][:], in_=bank[:], func=IDENTITY, bias=bias[:, j : j + 1], scale=1.0
                )

        def extend(r, chain, i):
            if is_round(r):
                j = chain[i]
                bank = form(r, j)
                longer = partial()
                nc.vector.scalar_tensor_tensor(
                    out=longer[:], in0=bank[:], scalar=bias[:, j : j + 1], in1=chains[(r, chain)][:], op0=ADD, op1=MULT
                )
                chains[(r, chain)] = longer

        def join_short_chains(r):
            if is_round(r):
                joined = partial()
                nc.gpsimd.tensor_tensor(
                    out=joined[:], in0=chains[(r, CHAIN_B)][:], in1=chains[(r, CHAIN_C)][:], op=MULT
                )
                chains[(r, CHAIN_B)] = joined

        def join_all(r):
            if is_round(r):
                result = stage.tile([P, ROUND], F32, bufs=BEHIND + 2)
                nc.gpsimd.tensor_tensor(
                    out=result[:], in0=chains[(r, CHAIN_B)][:], in1=chains[(r, CHAIN_A)][:], op=MULT
                )
                results[r] = result

        def transpose_result(r):
            if is_round(r):
                backs[r] = next_bank()
                for a in range(ROUND_BLOCKS):
                    cols = slice(a * P, (a + 1) * P)
                    nc.tensor.transpose(backs[r][:, cols], results[r][:, cols], identity[:])

        def store_result(r):
            if is_round(r):
                out_sb = stage.tile([P, ROUND], F32, bufs=3)
                if r % 2 == 0:
                    nc.scalar.copy(out=out_sb[:], in_=backs[r][:])
                else:
                    nc.vector.tensor_copy(out=out_sb[:], in_=backs[r][:])
                nc.sync.dma_start(out=out_rounds[r], in_=out_sb[:])

        w_codes = keep.tile([P, FORMS * P], U32, align_bytes=64)
        w_scales = keep.tile([P, FORMS * P], U8, align_bytes=64)
        w_grouped = []
        quantise_lag = 2

        def quantise_weights(pair):
            cols = slice(pair * PAIR_ROWS, (pair + 1) * PAIR_ROWS)
            nc.vector.quantize_mx(
                out=w_codes[:, cols].bitcast(FP8X4), scales=w_scales[:, cols], in_=w_grouped[pair][:]
            )

        transpose_state(0)
        regroup_state(0)
        for pair in range(WEIGHT_PAIRS):
            masked = keep.tile([P, PAIR * E], BF16, name="masked_%d" % pair)
            nc.vector.tensor_tensor(out=masked[:], in0=wg_sb[pair][:], in1=mg_sb[pair][:], op=MULT)
            if pair == 0:
                quantise_state(0)
            grouped = keep.tile([P, PAIR_ROWS * 4], BF16, align_bytes=64, name="w_grouped_%d" % pair)
            regroup_pair(transpose_pair(masked[:].bitcast(F32)), grouped[:])
            w_grouped.append(grouped)
            if pair >= quantise_lag:
                quantise_weights(pair - quantise_lag)
        for pair in range(WEIGHT_PAIRS - quantise_lag, WEIGHT_PAIRS):
            quantise_weights(pair)
        for r in range(1, AHEAD - 1):
            transpose_state(r)
            regroup_state(r)
            quantise_state(r)

        for t in range(-1, ROUNDS + BEHIND):
            extend(t, CHAIN_C, 1)
            if t >= 0:
                quantise_state(t + AHEAD - 1)
            join_short_chains(t)
            begin(t + 1, CHAIN_A)
            extend(t, CHAIN_A, 3)
            join_all(t)
            begin(t + 1, CHAIN_B)
            extend(t + 1, CHAIN_A, 1)
            begin(t + 1, CHAIN_C)
            extend(t + 1, CHAIN_B, 1)
            transpose_result(t - BEHIND)
            transpose_state(t + AHEAD)
            store_result(t - BEHIND)
            regroup_state(t + AHEAD)
            extend(t + 1, CHAIN_A, 2)
